import numpy as np
import ml_dtypes


def mxq(x, axis, fmt="e4m3"):
    dtype, down = {"e4m3": (ml_dtypes.float8_e4m3fn, 7), "e5m2": (ml_dtypes.float8_e5m2, 14)}[fmt]
    v = np.moveaxis(np.asarray(x, np.float32).astype(ml_dtypes.bfloat16).astype(np.float64), axis, -1)
    blocks = v.reshape(v.shape[:-1] + (-1, 32))
    amax = np.abs(blocks).max(-1, keepdims=True)
    byte = np.maximum(np.where(amax > 0, np.frexp(amax)[1] - 1 + 127, 0) - down, 1)
    scale = np.exp2(byte - 127.0)
    codes = (blocks / scale).astype(np.float32).astype(dtype).astype(np.float64)
    return np.moveaxis((codes * scale).reshape(v.shape), -1, axis)


WIDE = False


def mx_kscale(k):
    if not WIDE:
        return np.ones(k)
    levels = np.array([10, -10, 5, -5, 0])
    if k % 512:
        return np.exp2(np.random.permutation(np.resize(levels, k // 32))).repeat(32)
    a = np.empty((k // 512, 16))
    for p in range(k // 512):
        a[p, :8] = np.random.permutation(np.resize(levels, 8))
        for g in range(8):
            far = levels[np.abs(levels - a[p, g]) >= 10]
            a[p, g + 8] = far[np.random.randint(len(far))]
    return np.exp2(a.ravel()).repeat(32)


BF16 = ml_dtypes.bfloat16


def bf(x):
    return np.asarray(x, np.float32).astype(BF16)


def f64(x):
    return np.asarray(x).astype(np.float64)


N, M, D = 1024, 4096, 512


def sq_dist(X, SV):
    x2 = np.sum(X * X, axis=1)
    sv2 = np.sum(SV * SV, axis=1)
    return np.maximum(x2[:, None] + sv2[None, :] - 2.0 * (X @ SV.T), 0.0)


def setup_inputs():
    a = 0.7 / D ** 0.25
    s = mx_kscale(N)
    u = mx_kscale(M)
    u = u / np.min(u)
    X0 = bf(np.random.standard_normal((N, D)) * a)
    SV0 = bf(np.random.standard_normal((M, D)) * a)
    DC0 = bf(np.random.standard_normal((1, M)) * 8.0 / np.sqrt(M))
    IC = bf(np.random.standard_normal(1))
    gamma = bf((2.0 + 0.1 * np.random.standard_normal(1)) / np.sqrt(D))
    g = bf(np.random.standard_normal(N) * np.exp2(np.random.randint(-6, 1, N)) * 256.0 / s)
    d2 = sq_dist(f64(X0), f64(SV0))
    dec = np.sum(np.exp(-f64(gamma) * d2) * f64(DC0), axis=1)
    return {"X": bf(f64(X0) * s[:, None]),
            "SV": bf(f64(SV0) / u[:, None]),
            "DC": bf(f64(DC0) * u[None, :]),
            "IC": IC,
            "gamma": gamma,
            "d2": np.asarray(d2, np.float32),
            "dec": np.asarray(dec, np.float32),
            "grad_out": g}


def reference(X, SV, DC, IC, gamma, d2, dec, grad_out):
    Xf, SVf, gm, g = f64(X), f64(SV), f64(gamma), f64(grad_out)
    P = (2.0 * gm * g)[:, None] * f64(DC) * np.exp(-gm * f64(d2))
    r = 2.0 * gm * g * f64(dec)
    c = np.sum(P, axis=0)
    dX = (mxq(P, 1, "e5m2") @ mxq(SVf, 0, "e4m3")) - Xf * r[:, None]
    dSV = (mxq(P, 0, "e5m2").T @ mxq(Xf, 0, "e4m3")) - SVf * c[:, None]
    return dX, dSV

@@ -1,0 +1,441 @@
+from contextlib import ExitStack
+
+import concourse.mybir as mybir
+from concourse.masks import make_identity
+
+N, M, D = 1024, 4096, 512
+P = 128
+PACK = 4
+KP = P * PACK
+GH = N // KP
+GM = M // KP
+FLOPS = 2 * 2 * N * M * D
+
+F32 = mybir.dt.float32
+BF16 = mybir.dt.bfloat16
+U32 = mybir.dt.uint32
+U8 = mybir.dt.uint8
+E4 = mybir.dt.float8_e4m3fn_x4
+E5 = mybir.dt.float8_e5m2_x4
+ALU = mybir.AluOpType
+ACT = mybir.ActivationFunctionType
+
+
+def tile_rbf_svm_v_kernel(tc, X, SV, DC, IC, gamma, d2, dec, grad_out, out_0, out_1):
+    nc = tc.nc
+    d2_v = d2.rearrange("(h p t) m -> h p t m", p=P, t=PACK)
+    x_v = X.rearrange("(h p t) d -> h p t d", p=P, t=PACK)
+    sv_v = SV.rearrange("(g p j) d -> g p j d", p=P, j=PACK)
+    out0_v = out_0.rearrange("(h p t) d -> h p t d", p=P, t=PACK)
+    out1_v = out_1.rearrange("(g p j) d -> g p j d", p=P, j=PACK)
+
+    with ExitStack() as ctx:
+        keep = ctx.enter_context(tc.tile_pool(name="keep", bufs=1))
+        epool = ctx.enter_context(tc.tile_pool(name="epool", bufs=7))
+        work = ctx.enter_context(tc.tile_pool(name="work", bufs=3))
+        outs = ctx.enter_context(tc.tile_pool(name="outs", bufs=2))
+        small = ctx.enter_context(tc.tile_pool(name="small", bufs=4))
+        tpsum = ctx.enter_context(tc.psum_pool(name="tpsum", bufs=3))
+        cpsum = ctx.enter_context(tc.psum_pool(name="cpsum", bufs=1))
+        apsum = ctx.enter_context(tc.psum_pool(name="apsum", bufs=3))
+        dpsum = ctx.enter_context(tc.psum_pool(name="dpsum", bufs=1))
+        ctx.enter_context(tc.manual_schedule())
+
+        e = {}
+        dcp = {}
+        svraw = {}
+
+        def load_d2(k, pieces=1):
+            g, h = divmod(k, GH)
+            et = epool.tile([P, PACK, KP], F32, name="e")
+            step = PACK // pieces
+            for i in range(0, PACK, step):
+                nc.sync.dma_start(out=et[:, i : i + step, :], in_=d2_v[h][:, i : i + step, g * KP : (g + 1) * KP])
+            e[k] = et
+
+        dc_row = [keep.tile([P, 2 * KP], BF16, name="dc_row0"), keep.tile([P, 2 * KP], BF16, name="dc_row1")]
+        ones = keep.tile([P, P], BF16, name="ones")
+
+        def load_dc(q):
+            nc.gpsimd.dma_start(out=dc_row[q % 2][0:1, :], in_=DC[0:1, q * 2 * KP : (q + 1) * 2 * KP])
+
+        def spread_dc(q):
+            t = dpsum.tile([P, 2 * KP], BF16, name="dcp")
+            for x in range(2):
+                cs = slice(x * KP, (x + 1) * KP)
+                nc.tensor.matmul(t[:, cs], lhsT=ones[:], rhs=dc_row[q % 2][:, cs], start=True, stop=True)
+            dcp[q] = t
+
+        def load_sv(g):
+            t = work.tile([P, PACK, D], BF16, name="svraw", bufs=4)
+            nc.sync.dma_start(out=t[:], in_=sv_v[g])
+            svraw[g] = t
+
+        g_raw = keep.tile([P, GH, PACK], BF16, name="g_raw")
+        gam_raw = keep.tile([P, 1], BF16, name="gam_raw")
+        dec_sb = keep.tile([P, GH, PACK], F32, name="dec_sb")
+        dc_raw = keep.tile([P, GM, PACK], BF16, name="dc_raw")
+        nc.scalar.dma_start(out=gam_raw[:], in_=gamma.partition_broadcast(P))
+        nc.scalar.dma_start(out=g_raw[:], in_=grad_out.rearrange("(h p t) -> p h t", p=P, t=PACK))
+        load_d2(0, 4)
+        nc.vector.memset(dc_row[0][:], 0.0)
+        nc.vector.memset(dc_row[1][:], 0.0)
+        nc.vector.memset(ones[:], 1.0)
+        load_dc(0)
+        load_dc(1)
+        x_raw = keep.tile([P, GH, PACK, D], BF16, name="x_raw")
+        load_d2(1, 2)
+        load_d2(2)
+        for h in range(GH):
+            nc.sync.dma_start(out=x_raw[:, h], in_=x_v[h])
+        load_sv(0)
+        load_sv(1)
+        nc.gpsimd.dma_start(out=dec_sb[:], in_=dec.rearrange("(h p t) -> p h t", p=P, t=PACK))
+        nc.gpsimd.dma_start(out=dc_raw[:], in_=DC[0].rearrange("(g p j) -> p g j", p=P, j=PACK))
+
+        warm = keep.tile([P, 1], F32, name="warm")
+        nc.vector.memset(warm[:], 1.0)
+        warm2 = keep.tile([P, 1], F32, name="warm2")
+        nc.scalar.activation(out=warm2[:], in_=warm[:], func=ACT.Ln)
+        ident = keep.tile([P, P], F32, name="ident")
+        make_identity(nc, ident[:])
+        spread_dc(0)
+
+        nt = GH * PACK
+        gam = keep.tile([P, 1], F32, name="gam")
+        neg_gam = keep.tile([P, 1], F32, name="neg_gam")
+        nc.vector.tensor_copy(out=gam[:], in_=gam_raw[:])
+        nc.vector.tensor_scalar(out=neg_gam[:], in0=gam[:], scalar1=-1.0, scalar2=None, op0=ALU.mult)
+        s = keep.tile([P, nt], F32, name="s")
+        nc.vector.tensor_scalar(
+            out=s[:], in0=g_raw[:].rearrange("p h t -> p (h t)"), scalar1=gam[:, 0:1], scalar2=2.0, op0=ALU.mult, op1=ALU.mult
+        )
+        sgn2 = keep.tile([P, nt], F32, name="sgn2")
+        nc.vector.tensor_scalar(out=sgn2[:], in0=s[:], scalar1=0.0, scalar2=2.0, op0=ALU.is_ge, op1=ALU.mult)
+        sgn = keep.tile([P, nt], F32, name="sgn")
+        nc.vector.tensor_scalar(out=sgn[:], in0=sgn2[:], scalar1=-1.0, scalar2=None, op0=ALU.add)
+        s_abs = keep.tile([P, nt], F32, name="s_abs")
+        nc.vector.tensor_tensor(out=s_abs[:], in0=s[:], in1=sgn[:], op=ALU.mult)
+        s_pos = keep.tile([P, nt], F32, name="s_pos")
+        nc.vector.tensor_scalar(out=s_pos[:], in0=s_abs[:], scalar1=1e-19, scalar2=None, op0=ALU.max)
+        ln_s = keep.tile([P, nt], F32, name="ln_s")
+        nc.scalar.activation(out=ln_s[:], in_=s_pos[:], func=ACT.Ln)
+        nc.scalar.activation(out=warm2[:], in_=warm[:], func=ACT.Exp)
+
+        ind = keep.tile([P, PACK], F32, name="ind")
+        nc.vector.tensor_reduce(out=ind[:], in_=ident[:].rearrange("p (q j) -> p j q", j=PACK), axis=mybir.AxisListType.X, op=ALU.add)
+        sel = keep.tile([P, PACK, 32], F32, name="sel")
+        for b in range(PACK):
+            nc.vector.tensor_reduce(
+                out=sel[:, b],
+                in_=ident[:].rearrange("p (q j) -> p q j", j=PACK),
+                axis=mybir.AxisListType.X,
+                op=ALU.add,
+            )
+
+        neg_r = keep.tile([P, nt], F32, name="neg_r")
+        neg_s = keep.tile([P, nt], F32, name="neg_s")
+        nc.vector.tensor_scalar(out=neg_s[:], in0=s[:], scalar1=-1.0, scalar2=None, op0=ALU.mult)
+        nc.vector.tensor_tensor(out=neg_r[:], in0=neg_s[:], in1=dec_sb[:].rearrange("p h t -> p (h t)"), op=ALU.mult)
+        neg_dc = keep.tile([P, GM, PACK], F32, name="neg_dc")
+        nc.vector.tensor_scalar(out=neg_dc[:], in0=dc_raw[:], scalar1=-1.0, scalar2=None, op0=ALU.mult)
+
+        blk = keep.tile([P, PACK], F32, name="blk")
+        nc.vector.tensor_reduce(out=blk[:], in_=ident[:].rearrange("p (b q) -> p b q", b=PACK), axis=mybir.AxisListType.X, op=ALU.add)
+        ndm = keep.tile([P, GM, PACK, PACK], F32, name="ndm")
+        nc.vector.tensor_tensor(
+            out=ndm[:],
+            in0=neg_dc[:].unsqueeze(3).to_broadcast([P, GM, PACK, PACK]),
+            in1=blk[:].unsqueeze(1).unsqueeze(1).to_broadcast([P, GM, PACK, PACK]),
+            op=ALU.mult,
+        )
+
+        acc = keep.tile([P, nt, D], F32, name="acc")
+        for i in range(nt):
+            h, t = divmod(i, PACK)
+            nc.gpsimd.tensor_scalar(
+                out=acc[:, i], in0=x_raw[:, h, t], scalar1=neg_r[:, i : i + 1], scalar2=0.0, op0=ALU.mult, op1=ALU.add
+            )
+
+        xc = keep.tile([P, GH, D], U32, name="xc", align_bytes=64)
+        xs = keep.tile([P, GH, D], U8, name="xs", align_bytes=64)
+        svc = keep.tile([P, GM, D], U32, name="svc", align_bytes=64)
+        svs = keep.tile([P, GM, D], U8, name="svs", align_bytes=64)
+        ptc = keep.tile([P, GM * GH, KP], U32, name="ptc", align_bytes=64)
+        pts = keep.tile([P, GM * GH, KP], U8, name="pts", align_bytes=64)
+
+        xg = {}
+
+        def x_group(h):
+            t = work.tile([P, D, PACK], BF16, name="xg", align_bytes=64, bufs=1)
+            nc.vector.tensor_tensor(
+                out=t[:].rearrange("p (c i) t -> p c t i", i=4),
+                in0=x_raw[:, h].rearrange("p t (c i) -> p c t i", i=4),
+                in1=sgn[:, h * PACK : (h + 1) * PACK].unsqueeze(1).unsqueeze(3).to_broadcast([P, D // 4, PACK, 4]),
+                op=ALU.mult,
+            )
+            xg[h] = t
+
+        def x_quant(h):
+            nc.vector.quantize_mx(
+                out=xc[:, h].bitcast(E4), scales=xs[:, h], in_=xg[h][:].rearrange("p d t -> p (d t)")
+            )
+
+        svg = {}
+
+        def sv_group(g, half):
+            if half == 0:
+                t = work.tile([P, D, PACK], BF16, name="grp", align_bytes=64, bufs=2)
+                svg[g] = t
+            ds = slice(half * (D // 2), (half + 1) * (D // 2))
+            nc.scalar.copy(
+                out=svg[g][:, ds, :].rearrange("p (c i) j -> p c j i", i=4),
+                in_=svraw[g][:, :, ds].rearrange("p j (c i) -> p c j i", i=4),
+            )
+
+        def sv_quant(g):
+            nc.vector.quantize_mx(
+                out=svc[:, g].bitcast(E4), scales=svs[:, g], in_=svg[g][:].rearrange("p d j -> p (d j)")
+            )
+
+        def exp(k):
+            h = k % GH
+            for t in range(PACK):
+                i = h * PACK + t
+                nc.scalar.activation(
+                    out=e[k][:, t, :], in_=e[k][:, t, :], func=ACT.Exp, scale=neg_gam[:, 0:1], bias=ln_s[:, i : i + 1]
+                )
+
+        pb = {}
+
+        def form_p(k):
+            g = k // GH
+            t = work.tile([P, PACK, P, PACK], BF16, name="pb", align_bytes=64)
+            for q in range(2):
+                ms = slice(q * 64, (q + 1) * 64)
+                nc.vector.tensor_tensor(
+                    out=t[:, :, ms, :].rearrange("p j m t -> p m t j"),
+                    in0=e[k][:].rearrange("p t (m j) -> p m t j", j=PACK)[:, ms],
+                    in1=dcp[g // 2][:, (g % 2) * KP : (g % 2 + 1) * KP].rearrange("p (m j) -> p m j", j=PACK)[:, ms].unsqueeze(2).to_broadcast([P, 64, PACK, PACK]),
+                    op=ALU.mult,
+                )
+            pb[k] = t
+
+        def sign(k):
+            h = k % GH
+            for t in range(PACK):
+                i = h * PACK + t
+                nc.gpsimd.tensor_scalar(
+                    out=e[k][:, t, :], in0=e[k][:, t, :], scalar1=sgn[:, i : i + 1], scalar2=0.0, op0=ALU.mult, op1=ALU.add
+                )
+
+        pc, ps = {}, {}
+
+        def p_quant(k):
+            c = work.tile([P, KP], U32, name="pc", align_bytes=64, bufs=6)
+            sc = work.tile([P, KP], U8, name="ps", align_bytes=64, bufs=6)
+            nc.vector.quantize_mx(out=c[:].bitcast(E5), scales=sc[:], in_=pb[k][:].rearrange("p j m t -> p (j m t)"))
+            pc[k], ps[k] = c, sc
+
+        tp = {}
+
+        def turn(k):
+            words = pb[k][:].rearrange("p j m t -> p (j m t)").bitcast(F32)
+            for u in range(2):
+                t = tpsum.tile([P, PACK, P], F32, name="tp")
+                for j in range(PACK):
+                    nc.tensor.transpose(t[:, j, :], words[:, 2 * P * j + u : 2 * P * (j + 1) : 2], ident[:])
+                tp[k, u] = t
+
+        pt = {}
+
+        def evac(k):
+            o = work.tile([P, PACK, P, PACK], BF16, name="pt", align_bytes=64, bufs=2)
+            for u in range(2):
+                nc.scalar.copy(
+                    out=o[:, 2 * u : 2 * u + 2],
+                    in_=tp[k, u][:].rearrange("q j p -> q (j p)").bitcast(BF16).rearrange("q (j p e) -> q e p j", j=PACK, e=2),
+                )
+            pt[k] = o
+
+        def pt_quant(k):
+            nc.vector.quantize_mx(
+                out=ptc[:, k].bitcast(E5), scales=pts[:, k], in_=pt[k][:].rearrange("q t p j -> q (t p j)")
+            )
+
+        cps = {}
+
+        def c_sum(g):
+            t = cpsum.tile([P, PACK, P], F32, name="cps")
+            for b in range(PACK):
+                for i in range(nt):
+                    h, tt = divmod(i, PACK)
+                    nc.tensor.matmul(
+                        t[:, b],
+                        lhsT=e[g * GH + h][:, tt, b * P : (b + 1) * P],
+                        rhs=ident[:],
+                        start=(i == 0),
+                        stop=(i == nt - 1),
+                        is_transpose=True,
+                    )
+            cps[g] = t
+
+        cm = {}
+
+        def c_mask(g):
+            cs = small.tile([P, PACK], F32, name="cs")
+            nc.vector.tensor_reduce(out=cs[:], in_=cps[g][:], axis=mybir.AxisListType.X, op=ALU.add)
+            t = small.tile([P, PACK, PACK], F32, name="cm")
+            nc.vector.tensor_tensor(
+                out=t[:],
+                in0=cs[:].unsqueeze(2).to_broadcast([P, PACK, PACK]),
+                in1=ind[:].unsqueeze(1).to_broadcast([P, PACK, PACK]),
+                op=ALU.mult,
+            )
+            cm[g] = t
+
+        def c_move(g):
+            nc.tensor.matmul(
+                cps[g][:, 0, 0 : PACK * PACK],
+                lhsT=sel[:].rearrange("p b q -> p (b q)"),
+                rhs=cm[g][:].rearrange("p b j -> p (b j)"),
+                start=True,
+                stop=True,
+            )
+
+        negc = {}
+
+        def c_neg(g):
+            w = small.tile([P, PACK, PACK], F32, name="cw")
+            nc.vector.tensor_tensor(
+                out=w[:],
+                in0=cps[g][:, 0, 0 : PACK * PACK].rearrange("p (b j) -> p j b", b=PACK),
+                in1=ndm[:, g],
+                op=ALU.mult,
+            )
+            t = small.tile([P, PACK], F32, name="negc")
+            nc.vector.tensor_reduce(out=t[:], in_=w[:], axis=mybir.AxisListType.X, op=ALU.add)
+            negc[g] = t
+
+        m1 = {}
+
+        def mx1(g, j):
+            t = apsum.tile([P, D], F32, name="bank")
+            js = slice(j * P, (j + 1) * P)
+            for h in range(GH):
+                k = g * GH + h
+                nc.tensor.matmul_mx(
+                    out=t[:],
+                    lhsT=pc[k][:, js].bitcast(E5),
+                    lhsT_scale=ps[k][:, js],
+                    rhs=xc[:, h].bitcast(E4),
+                    rhs_scale=xs[:, h],
+                    start=(h == 0),
+                    stop=(h == GH - 1),
+                )
+            m1[g, j] = t
+
+        def out1(g, pair):
+            o = outs.tile([P, 2, D], F32, name="o1")
+            for x in range(2):
+                j = 2 * pair + x
+                nc.vector.scalar_tensor_tensor(
+                    out=o[:, x], in0=svraw[g][:, j], scalar=negc[g][:, j : j + 1], in1=m1[g, j][:], op0=ALU.mult, op1=ALU.add
+                )
+            nc.sync.dma_start(out=out1_v[g][:, 2 * pair : 2 * pair + 2], in_=o[:])
+
+        m0 = {}
+
+        def mx0(i, gs, start, stop):
+            h, tt = divmod(i, PACK)
+            if start:
+                t = apsum.tile([P, D], F32, name="bank")
+                m0[i] = t
+            ts = slice(tt * P, (tt + 1) * P)
+            for n, g in enumerate(gs):
+                k = g * GH + h
+                nc.tensor.matmul_mx(
+                    out=m0[i][:],
+                    lhsT=ptc[:, k, ts].bitcast(E5),
+                    lhsT_scale=pts[:, k, ts],
+                    rhs=svc[:, g].bitcast(E4),
+                    rhs_scale=svs[:, g],
+                    start=(start and n == 0),
+                    stop=(stop and n == len(gs) - 1),
+                )
+
+        def sweep(i):
+            nc.vector.scalar_tensor_tensor(
+                out=acc[:, i], in0=m0[i][:], scalar=sgn[:, i : i + 1], in1=acc[:, i], op0=ALU.mult, op1=ALU.add
+            )
+
+        def out0(i):
+            h, tt = divmod(i, PACK)
+            o = outs.tile([P, D], F32, name="o0")
+            nc.vector.scalar_tensor_tensor(
+                out=o[:], in0=m0[i][:], scalar=sgn[:, i : i + 1], in1=acc[:, i], op0=ALU.mult, op1=ALU.add
+            )
+            nc.sync.dma_start(out=out0_v[h][:, tt], in_=o[:])
+
+        K = GM * GH
+        SPLIT = [4, 4, 4, 4, 5, 5, 5, 5]
+        first = {10: 0, 11: 1, 12: 2, 13: 3, 14: 4, 15: 5, 16: 6, 17: 7}
+
+        for st in range(K + 4):
+            odd = st % 2 == 1
+            ga = (st - 4) // 2
+            gb = (st - 5) // 2
+            gc = (st - 3) // 2
+            if st + 3 < K:
+                load_d2(st + 3)
+            if odd and (st + 3) // 2 < GM:
+                load_sv((st + 3) // 2)
+            if st % 4 == 2 and (st + 6) // 4 < GM // 2:
+                load_dc((st + 6) // 4)
+            if st < K:
+                exp(st)
+            if not odd and 0 <= ga < GM:
+                c_mask(ga)
+            if 1 <= st <= K:
+                form_p(st - 1)
+                sign(st - 1)
+            if st in (1, 2):
+                x_group(st - 1)
+            if not odd and 0 <= ga < GM:
+                mx1(ga, 0)
+                mx1(ga, 1)
+                c_move(ga)
+            if odd and 0 <= gb < GM:
+                mx1(gb, 2)
+                mx1(gb, 3)
+            if st in first:
+                i = first[st]
+                mx0(i, list(range(SPLIT[i])), True, True)
+            if 3 <= st < K + 3:
+                pt_quant(st - 3)
+            if not odd and 0 <= ga < GM:
+                c_neg(ga)
+                out1(ga, 0)
+            if odd and 0 <= gb < GM:
+                out1(gb, 1)
+            if st in first:
+                sweep(first[st])
+            if st % 4 == 0 and 0 < st < K:
+                spread_dc(st // 4)
+            if 1 <= st <= K:
+                turn(st - 1)
+            if odd and 0 <= gc < GM:
+                c_sum(gc)
+            if 2 <= st <= K + 1:
+                evac(st - 2)
+            if 1 <= st <= K:
+                p_quant(st - 1)
+            if st in (1, 2):
+                x_quant(st - 1)
+            if 0 <= st - 1 < K:
+                sv_group((st - 1) // 2, (st - 1) % 2)
+            if odd and 0 <= st - 3 < K:
+                sv_quant((st - 3) // 2)
+        for i in range(nt):
+            mx0(i, list(range(SPLIT[i], GM)), True, True)
+            out0(i)

@@ -54,6 +54,8 @@ def tile_rbf_svm_v_kernel(tc, X, SV, DC, IC, gamma, d2, dec, grad_out, out_0, ou
             e[k] = et
 
         dc_row = [keep.tile([P, 2 * KP], BF16, name="dc_row0"), keep.tile([P, 2 * KP], BF16, name="dc_row1")]
+        dc_head = keep.tile([P, 2 * KP], BF16, name="dc_head")
+        dcp[0] = dc_head
         ones = keep.tile([P, P], BF16, name="ones")
 
         def load_dc(q):
@@ -77,21 +79,17 @@ def tile_rbf_svm_v_kernel(tc, X, SV, DC, IC, gamma, d2, dec, grad_out, out_0, ou
         dc_raw = keep.tile([P, GM, PACK], BF16, name="dc_raw")
         nc.scalar.dma_start(out=gam_raw[:], in_=gamma.partition_broadcast(P))
         nc.scalar.dma_start(out=g_raw[:], in_=grad_out.rearrange("(h p t) -> p h t", p=P, t=PACK))
-        load_d2(0, 4)
-        nc.vector.memset(dc_row[0][:], 0.0)
-        nc.vector.memset(dc_row[1][:], 0.0)
-        nc.vector.memset(ones[:], 1.0)
-        load_dc(0)
-        load_dc(1)
-        x_raw = keep.tile([P, GH, PACK, D], BF16, name="x_raw")
-        load_d2(1, 2)
-        load_d2(2)
-        for h in range(GH):
-            nc.sync.dma_start(out=x_raw[:, h], in_=x_v[h])
-        load_sv(0)
-        load_sv(1)
         nc.gpsimd.dma_start(out=dec_sb[:], in_=dec.rearrange("(h p t) -> p h t", p=P, t=PACK))
         nc.gpsimd.dma_start(out=dc_raw[:], in_=DC[0].rearrange("(g p j) -> p g j", p=P, j=PACK))
+        nc.scalar.dma_start(out=dc_head[:], in_=DC[0, 0 : 2 * KP].partition_broadcast(P))
+        load_d2(0, 4)
+        x_raw = keep.tile([P, GH, PACK, D], BF16, name="x_raw")
+        nc.sync.dma_start(out=x_raw[:, 0], in_=x_v[0])
+        load_d2(1, 2)
+        nc.sync.dma_start(out=x_raw[:, 1], in_=x_v[1])
+        load_d2(2)
+        load_sv(0)
+        load_sv(1)
 
         warm = keep.tile([P, 1], F32, name="warm")
         nc.vector.memset(warm[:], 1.0)
@@ -99,32 +97,15 @@ def tile_rbf_svm_v_kernel(tc, X, SV, DC, IC, gamma, d2, dec, grad_out, out_0, ou
         nc.scalar.activation(out=warm2[:], in_=warm[:], func=ACT.Ln)
         ident = keep.tile([P, P], F32, name="ident")
         make_identity(nc, ident[:])
-        spread_dc(0)
-
-        nt = GH * PACK
-        gam = keep.tile([P, 1], F32, name="gam")
-        neg_gam = keep.tile([P, 1], F32, name="neg_gam")
-        nc.vector.tensor_copy(out=gam[:], in_=gam_raw[:])
-        nc.vector.tensor_scalar(out=neg_gam[:], in0=gam[:], scalar1=-1.0, scalar2=None, op0=ALU.mult)
-        s = keep.tile([P, nt], F32, name="s")
-        nc.vector.tensor_scalar(
-            out=s[:], in0=g_raw[:].rearrange("p h t -> p (h t)"), scalar1=gam[:, 0:1], scalar2=2.0, op0=ALU.mult, op1=ALU.mult
-        )
-        sgn2 = keep.tile([P, nt], F32, name="sgn2")
-        nc.vector.tensor_scalar(out=sgn2[:], in0=s[:], scalar1=0.0, scalar2=2.0, op0=ALU.is_ge, op1=ALU.mult)
-        sgn = keep.tile([P, nt], F32, name="sgn")
-        nc.vector.tensor_scalar(out=sgn[:], in0=sgn2[:], scalar1=-1.0, scalar2=None, op0=ALU.add)
-        s_abs = keep.tile([P, nt], F32, name="s_abs")
-        nc.vector.tensor_tensor(out=s_abs[:], in0=s[:], in1=sgn[:], op=ALU.mult)
-        s_pos = keep.tile([P, nt], F32, name="s_pos")
-        nc.vector.tensor_scalar(out=s_pos[:], in0=s_abs[:], scalar1=1e-19, scalar2=None, op0=ALU.max)
-        ln_s = keep.tile([P, nt], F32, name="ln_s")
-        nc.scalar.activation(out=ln_s[:], in_=s_pos[:], func=ACT.Ln)
-        nc.scalar.activation(out=warm2[:], in_=warm[:], func=ACT.Exp)
-
+        nc.gpsimd.memset(ones[:], 1.0)
+        nc.gpsimd.memset(dc_row[1][:], 0.0)
+        nc.gpsimd.memset(dc_row[0][:], 0.0)
+        load_dc(1)
+        load_dc(2)
         ind = keep.tile([P, PACK], F32, name="ind")
-        nc.vector.tensor_reduce(out=ind[:], in_=ident[:].rearrange("p (q j) -> p j q", j=PACK), axis=mybir.AxisListType.X, op=ALU.add)
         sel = keep.tile([P, PACK, 32], F32, name="sel")
+        blk = keep.tile([P, PACK], F32, name="blk")
+        nc.vector.tensor_reduce(out=ind[:], in_=ident[:].rearrange("p (q j) -> p j q", j=PACK), axis=mybir.AxisListType.X, op=ALU.add)
         for b in range(PACK):
             nc.vector.tensor_reduce(
                 out=sel[:, b],
@@ -133,29 +114,54 @@ def tile_rbf_svm_v_kernel(tc, X, SV, DC, IC, gamma, d2, dec, grad_out, out_0, ou
                 op=ALU.add,
             )
 
+        nc.vector.tensor_reduce(out=blk[:], in_=ident[:].rearrange("p (b q) -> p b q", b=PACK), axis=mybir.AxisListType.X, op=ALU.add)
+
+
+        nt = GH * PACK
+        s = keep.tile([P, nt], F32, name="s")
+        nc.vector.tensor_scalar(
+            out=s[:], in0=g_raw[:].rearrange("p h t -> p (h t)"), scalar1=gam_raw[:, 0:1], scalar2=2.0, op0=ALU.mult, op1=ALU.mult
+        )
+        s_abs = keep.tile([P, nt], F32, name="s_abs")
+        nc.vector.scalar_tensor_tensor(out=s_abs[:], in0=s[:], scalar=-1.0, in1=s[:], op0=ALU.mult, op1=ALU.max)
+        neg_gam = keep.tile([P, 1], F32, name="neg_gam")
+        nc.vector.tensor_scalar(out=neg_gam[:], in0=gam_raw[:], scalar1=-1.0, scalar2=None, op0=ALU.mult)
+        s_pos = keep.tile([P, nt], F32, name="s_pos")
+        nc.vector.tensor_scalar(out=s_pos[:], in0=s_abs[:], scalar1=1e-19, scalar2=None, op0=ALU.max)
+        sgn2 = keep.tile([P, nt], F32, name="sgn2")
+        nc.vector.tensor_scalar(out=sgn2[:], in0=s[:], scalar1=0.0, scalar2=2.0, op0=ALU.is_ge, op1=ALU.mult)
+        sgn = keep.tile([P, nt], F32, name="sgn")
+        nc.vector.tensor_scalar(out=sgn[:], in0=sgn2[:], scalar1=-1.0, scalar2=None, op0=ALU.add)
+        ln_s = keep.tile([P, nt], F32, name="ln_s")
+        nc.scalar.activation(out=ln_s[:], in_=s_pos[:], func=ACT.Ln)
+        nc.scalar.activation(out=warm2[:], in_=warm[:], func=ACT.Exp)
+
         neg_r = keep.tile([P, nt], F32, name="neg_r")
         neg_s = keep.tile([P, nt], F32, name="neg_s")
-        nc.vector.tensor_scalar(out=neg_s[:], in0=s[:], scalar1=-1.0, scalar2=None, op0=ALU.mult)
-        nc.vector.tensor_tensor(out=neg_r[:], in0=neg_s[:], in1=dec_sb[:].rearrange("p h t -> p (h t)"), op=ALU.mult)
         neg_dc = keep.tile([P, GM, PACK], F32, name="neg_dc")
-        nc.vector.tensor_scalar(out=neg_dc[:], in0=dc_raw[:], scalar1=-1.0, scalar2=None, op0=ALU.mult)
-
-        blk = keep.tile([P, PACK], F32, name="blk")
-        nc.vector.tensor_reduce(out=blk[:], in_=ident[:].rearrange("p (b q) -> p b q", b=PACK), axis=mybir.AxisListType.X, op=ALU.add)
         ndm = keep.tile([P, GM, PACK, PACK], F32, name="ndm")
-        nc.vector.tensor_tensor(
-            out=ndm[:],
-            in0=neg_dc[:].unsqueeze(3).to_broadcast([P, GM, PACK, PACK]),
-            in1=blk[:].unsqueeze(1).unsqueeze(1).to_broadcast([P, GM, PACK, PACK]),
-            op=ALU.mult,
-        )
-
         acc = keep.tile([P, nt, D], F32, name="acc")
-        for i in range(nt):
-            h, t = divmod(i, PACK)
-            nc.gpsimd.tensor_scalar(
-                out=acc[:, i], in0=x_raw[:, h, t], scalar1=neg_r[:, i : i + 1], scalar2=0.0, op0=ALU.mult, op1=ALU.add
+
+        def constants2():
+            nc.vector.tensor_scalar(out=neg_s[:], in0=s[:], scalar1=-1.0, scalar2=None, op0=ALU.mult)
+            nc.vector.tensor_tensor(out=neg_r[:], in0=neg_s[:], in1=dec_sb[:].rearrange("p h t -> p (h t)"), op=ALU.mult)
+            nc.vector.tensor_scalar(out=neg_dc[:], in0=dc_raw[:], scalar1=-1.0, scalar2=None, op0=ALU.mult)
+
+            nc.vector.tensor_tensor(
+                out=ndm[:],
+                in0=neg_dc[:].unsqueeze(3).to_broadcast([P, GM, PACK, PACK]),
+                in1=blk[:].unsqueeze(1).unsqueeze(1).to_broadcast([P, GM, PACK, PACK]),
+                op=ALU.mult,
             )
+
+
+        def start_acc():
+            for i in range(nt):
+                h, t = divmod(i, PACK)
+                nc.gpsimd.tensor_scalar(
+                    out=acc[:, i], in0=x_raw[:, h, t], scalar1=neg_r[:, i : i + 1], scalar2=0.0, op0=ALU.mult, op1=ALU.add
+                )
+
 
         xc = keep.tile([P, GH, D], U32, name="xc", align_bytes=64)
         xs = keep.tile([P, GH, D], U8, name="xs", align_bytes=64)
@@ -371,7 +377,7 @@ def tile_rbf_svm_v_kernel(tc, X, SV, DC, IC, gamma, d2, dec, grad_out, out_0, ou
 
         def out0(i):
             h, tt = divmod(i, PACK)
-            o = outs.tile([P, D], F32, name="o0")
+            o = outs.tile([P, D], F32, name="o0", bufs=4)
             nc.vector.scalar_tensor_tensor(
                 out=o[:], in0=m0[i][:], scalar=sgn[:, i : i + 1], in1=acc[:, i], op0=ALU.mult, op1=ALU.add
             )
@@ -390,17 +396,23 @@ def tile_rbf_svm_v_kernel(tc, X, SV, DC, IC, gamma, d2, dec, grad_out, out_0, ou
                 load_d2(st + 3)
             if odd and (st + 3) // 2 < GM:
                 load_sv((st + 3) // 2)
-            if st % 4 == 2 and (st + 6) // 4 < GM // 2:
-                load_dc((st + 6) // 4)
+            if st == 6:
+                load_dc(3)
             if st < K:
                 exp(st)
-            if not odd and 0 <= ga < GM:
-                c_mask(ga)
+            if st == 0:
+                x_group(0)
+                x_quant(0)
             if 1 <= st <= K:
                 form_p(st - 1)
                 sign(st - 1)
-            if st in (1, 2):
-                x_group(st - 1)
+            if st == 1:
+                x_group(1)
+            if st == 2:
+                constants2()
+                start_acc()
+            if not odd and 0 <= ga < GM:
+                c_mask(ga)
             if not odd and 0 <= ga < GM:
                 mx1(ga, 0)
                 mx1(ga, 1)
@@ -430,8 +442,8 @@ def tile_rbf_svm_v_kernel(tc, X, SV, DC, IC, gamma, d2, dec, grad_out, out_0, ou
                 evac(st - 2)
             if 1 <= st <= K:
                 p_quant(st - 1)
-            if st in (1, 2):
-                x_quant(st - 1)
+            if st == 1:
+                x_quant(1)
             if 0 <= st - 1 < K:
                 sv_group((st - 1) // 2, (st - 1) % 2)
             if odd and 0 <= st - 3 < K:

@@ -9,6 +9,10 @@ PACK = 4
 KP = P * PACK
 GH = N // KP
 GM = M // KP
+SIGN = "gggs"
+CRED = "v"
+SWEEP = "vvvvvvvv"
+OUT0 = "vvvvvvvv"
 FLOPS = 2 * 2 * N * M * D
 
 F32 = mybir.dt.float32
@@ -155,12 +159,11 @@ def tile_rbf_svm_v_kernel(tc, X, SV, DC, IC, gamma, d2, dec, grad_out, out_0, ou
             )
 
 
-        def start_acc():
-            for i in range(nt):
-                h, t = divmod(i, PACK)
-                nc.gpsimd.tensor_scalar(
-                    out=acc[:, i], in0=x_raw[:, h, t], scalar1=neg_r[:, i : i + 1], scalar2=0.0, op0=ALU.mult, op1=ALU.add
-                )
+        def start_acc(i):
+            h, t = divmod(i, PACK)
+            nc.gpsimd.tensor_scalar(
+                out=acc[:, i], in0=x_raw[:, h, t], scalar1=neg_r[:, i : i + 1], scalar2=0.0, op0=ALU.mult, op1=ALU.add
+            )
 
 
         xc = keep.tile([P, GH, D], U32, name="xc", align_bytes=64)
@@ -227,13 +230,25 @@ def tile_rbf_svm_v_kernel(tc, X, SV, DC, IC, gamma, d2, dec, grad_out, out_0, ou
                 )
             pb[k] = t
 
-        def sign(k):
+        def sign(k, who):
             h = k % GH
+            if who == "g" and "g" in SIGN and k < GM * GH - 1:
+                gate = small.tile([P, 1], U32, name="gate")
+                nc.gpsimd.tensor_copy(out=gate[:], in_=pc[k][:, 0:1])
             for t in range(PACK):
                 i = h * PACK + t
-                nc.gpsimd.tensor_scalar(
-                    out=e[k][:, t, :], in0=e[k][:, t, :], scalar1=sgn[:, i : i + 1], scalar2=0.0, op0=ALU.mult, op1=ALU.add
-                )
+                if SIGN[t] != who:
+                    continue
+                if who == "g":
+                    nc.gpsimd.tensor_scalar(
+                        out=e[k][:, t, :], in0=e[k][:, t, :], scalar1=sgn[:, i : i + 1], scalar2=0.0, op0=ALU.mult, op1=ALU.add
+                    )
+                elif who == "v":
+                    nc.vector.tensor_scalar(
+                        out=e[k][:, t, :], in0=e[k][:, t, :], scalar1=sgn[:, i : i + 1], scalar2=None, op0=ALU.mult
+                    )
+                else:
+                    nc.scalar.activation(out=e[k][:, t, :], in_=e[k][:, t, :], func=ACT.Copy, scale=sgn[:, i : i + 1])
 
         pc, ps = {}, {}
 
@@ -290,7 +305,12 @@ def tile_rbf_svm_v_kernel(tc, X, SV, DC, IC, gamma, d2, dec, grad_out, out_0, ou
 
         def c_mask(g):
             cs = small.tile([P, PACK], F32, name="cs")
-            nc.vector.tensor_reduce(out=cs[:], in_=cps[g][:], axis=mybir.AxisListType.X, op=ALU.add)
+            if CRED == "v":
+                nc.vector.tensor_reduce(out=cs[:], in_=cps[g][:], axis=mybir.AxisListType.X, op=ALU.add)
+            else:
+                junk = small.tile([P, P], F32, name="junk", bufs=1)
+                for b in range(PACK):
+                    nc.scalar.activation(out=junk[:], in_=cps[g][:, b], func=ACT.Copy, accum_out=cs[:, b : b + 1])
             t = small.tile([P, PACK, PACK], F32, name="cm")
             nc.vector.tensor_tensor(
                 out=t[:],
@@ -371,21 +391,32 @@ def tile_rbf_svm_v_kernel(tc, X, SV, DC, IC, gamma, d2, dec, grad_out, out_0, ou
                 )
 
         def sweep(i):
-            nc.vector.scalar_tensor_tensor(
-                out=acc[:, i], in0=m0[i][:], scalar=sgn[:, i : i + 1], in1=acc[:, i], op0=ALU.mult, op1=ALU.add
-            )
+            if SWEEP[i] == "v":
+                nc.vector.scalar_tensor_tensor(
+                    out=acc[:, i], in0=m0[i][:], scalar=sgn[:, i : i + 1], in1=acc[:, i], op0=ALU.mult, op1=ALU.add
+                )
+            else:
+                w = small.tile([P, D], F32, name="part", bufs=2)
+                nc.scalar.activation(out=w[:], in_=m0[i][:], func=ACT.Copy, scale=sgn[:, i : i + 1])
+                nc.gpsimd.tensor_tensor(out=acc[:, i], in0=acc[:, i], in1=w[:], op=ALU.add)
 
         def out0(i):
             h, tt = divmod(i, PACK)
             o = outs.tile([P, D], F32, name="o0", bufs=4)
-            nc.vector.scalar_tensor_tensor(
-                out=o[:], in0=m0[i][:], scalar=sgn[:, i : i + 1], in1=acc[:, i], op0=ALU.mult, op1=ALU.add
-            )
+            if OUT0[i] == "v":
+                nc.vector.scalar_tensor_tensor(
+                    out=o[:], in0=m0[i][:], scalar=sgn[:, i : i + 1], in1=acc[:, i], op0=ALU.mult, op1=ALU.add
+                )
+            else:
+                w = small.tile([P, D], F32, name="part", bufs=2)
+                nc.scalar.activation(out=w[:], in_=m0[i][:], func=ACT.Copy, scale=sgn[:, i : i + 1])
+                nc.gpsimd.tensor_tensor(out=o[:], in0=acc[:, i], in1=w[:], op=ALU.add)
             nc.sync.dma_start(out=out0_v[h][:, tt], in_=o[:])
 
         K = GM * GH
-        SPLIT = [4, 4, 4, 4, 5, 5, 5, 5]
-        first = {10: 0, 11: 1, 12: 2, 13: 3, 14: 4, 15: 5, 16: 6, 17: 7}
+        first = {10: 0, 11: 4, 12: 1, 13: 5, 14: 2, 15: 6, 16: 3, 17: 7}
+        split = {i: (st - 2 - i // PACK) // 2 for st, i in first.items()}
+        early = [0, 1]
 
         for st in range(K + 4):
             odd = st % 2 == 1
@@ -403,28 +434,34 @@ def tile_rbf_svm_v_kernel(tc, X, SV, DC, IC, gamma, d2, dec, grad_out, out_0, ou
             if st == 0:
                 x_group(0)
                 x_quant(0)
+            if st == K + 2:
+                for i in early:
+                    mx0(i, list(range(split[i], GM)), True, True)
+            if not odd and 0 <= ga < GM:
+                c_mask(ga)
+            if st == K + 2:
+                for i in early:
+                    out0(i)
             if 1 <= st <= K:
                 form_p(st - 1)
-                sign(st - 1)
             if st == 1:
                 x_group(1)
             if st == 2:
                 constants2()
-                start_acc()
             if not odd and 0 <= ga < GM:
-                c_mask(ga)
-            if not odd and 0 <= ga < GM:
+                c_move(ga)
                 mx1(ga, 0)
                 mx1(ga, 1)
-                c_move(ga)
             if odd and 0 <= gb < GM:
                 mx1(gb, 2)
                 mx1(gb, 3)
             if st in first:
                 i = first[st]
-                mx0(i, list(range(SPLIT[i])), True, True)
-            if 3 <= st < K + 3:
-                pt_quant(st - 3)
+                mx0(i, list(range(split[i])), True, True)
+            if 1 <= st <= K:
+                sign(st - 1, "v")
+            if odd and 0 <= gc < GM:
+                c_sum(gc)
             if not odd and 0 <= ga < GM:
                 c_neg(ga)
                 out1(ga, 0)
@@ -436,18 +473,24 @@ def tile_rbf_svm_v_kernel(tc, X, SV, DC, IC, gamma, d2, dec, grad_out, out_0, ou
                 spread_dc(st // 4)
             if 1 <= st <= K:
                 turn(st - 1)
-            if odd and 0 <= gc < GM:
-                c_sum(gc)
             if 2 <= st <= K + 1:
                 evac(st - 2)
             if 1 <= st <= K:
-                p_quant(st - 1)
+                sign(st - 1, "s")
             if st == 1:
                 x_quant(1)
-            if 0 <= st - 1 < K:
-                sv_group((st - 1) // 2, (st - 1) % 2)
+            if 3 <= st < K + 3:
+                pt_quant(st - 3)
             if odd and 0 <= st - 3 < K:
                 sv_quant((st - 3) // 2)
+            if 1 <= st <= K:
+                p_quant(st - 1)
+                sign(st - 1, "g")
+            if 2 <= st < 2 + nt:
+                start_acc(st - 2)
+            if 0 <= st - 1 < K:
+                sv_group((st - 1) // 2, (st - 1) % 2)
         for i in range(nt):
-            mx0(i, list(range(SPLIT[i], GM)), True, True)
-            out0(i)
+            if i not in early:
+                mx0(i, list(range(split[i], GM)), True, True)
+                out0(i)

@@ -9,10 +9,20 @@ PACK = 4
 KP = P * PACK
 GH = N // KP
 GM = M // KP
-SIGN = "gggs"
-CRED = "v"
-SWEEP = "vvvvvvvv"
-OUT0 = "vvvvvvvv"
+FOLDS = [0] * 3 + [1, 2] * 6 + [2]
+TB = 2
+AB = 4
+CB = 2
+EB = 5
+PCB = 6
+O0B = 4
+SVB = 4
+EARLY = 1
+SVG = "s"
+CRED = "s"
+ORDER = [("load", -3), ("loaddc", 0), ("c_sum0", 2), ("fold1", 2), ("x1", 3), ("mx1a", 4), ("c_copy", 4), ("sv_group", 4), ("mx1b", 4), ("const", 3), ("x0", 1), ("acc0", 3), ("evac", 2), ("mx0", 9), ("c_turn", 4), ("form_p", 1), ("sv_quant", 5), ("c_sum1", 2), ("exp", 0), ("p_quant", 2), ("c_neg", 4), ("fold0", 1), ("acc", 10), ("out1", 4), ("pt_quant", 3), ("turn0", 1), ("loadsv", -3), ("turn1", 1), ("c_early", 0)]
+TILES = [0, 4, 1, 5, 2, 6, 3, 7]
+LAST = [0, 1, 2, 3, 4, 5, 6, 7]
 FLOPS = 2 * 2 * N * M * D
 
 F32 = mybir.dt.float32
@@ -35,18 +45,16 @@ def tile_rbf_svm_v_kernel(tc, X, SV, DC, IC, gamma, d2, dec, grad_out, out_0, ou
 
     with ExitStack() as ctx:
         keep = ctx.enter_context(tc.tile_pool(name="keep", bufs=1))
-        epool = ctx.enter_context(tc.tile_pool(name="epool", bufs=7))
+        epool = ctx.enter_context(tc.tile_pool(name="epool", bufs=EB))
         work = ctx.enter_context(tc.tile_pool(name="work", bufs=3))
         outs = ctx.enter_context(tc.tile_pool(name="outs", bufs=2))
         small = ctx.enter_context(tc.tile_pool(name="small", bufs=4))
-        tpsum = ctx.enter_context(tc.psum_pool(name="tpsum", bufs=3))
-        cpsum = ctx.enter_context(tc.psum_pool(name="cpsum", bufs=1))
-        apsum = ctx.enter_context(tc.psum_pool(name="apsum", bufs=3))
-        dpsum = ctx.enter_context(tc.psum_pool(name="dpsum", bufs=1))
+        tpsum = ctx.enter_context(tc.psum_pool(name="tpsum", bufs=TB))
+        cpsum = ctx.enter_context(tc.psum_pool(name="cpsum", bufs=CB))
+        apsum = ctx.enter_context(tc.psum_pool(name="apsum", bufs=AB))
         ctx.enter_context(tc.manual_schedule())
 
         e = {}
-        dcp = {}
         svraw = {}
 
         def load_d2(k, pieces=1):
@@ -57,23 +65,14 @@ def tile_rbf_svm_v_kernel(tc, X, SV, DC, IC, gamma, d2, dec, grad_out, out_0, ou
                 nc.sync.dma_start(out=et[:, i : i + step, :], in_=d2_v[h][:, i : i + step, g * KP : (g + 1) * KP])
             e[k] = et
 
-        dc_row = [keep.tile([P, 2 * KP], BF16, name="dc_row0"), keep.tile([P, 2 * KP], BF16, name="dc_row1")]
-        dc_head = keep.tile([P, 2 * KP], BF16, name="dc_head")
-        dcp[0] = dc_head
-        ones = keep.tile([P, P], BF16, name="ones")
+        dcb = keep.tile([P, M], BF16, name="dcb")
 
         def load_dc(q):
-            nc.gpsimd.dma_start(out=dc_row[q % 2][0:1, :], in_=DC[0:1, q * 2 * KP : (q + 1) * 2 * KP])
-
-        def spread_dc(q):
-            t = dpsum.tile([P, 2 * KP], BF16, name="dcp")
-            for x in range(2):
-                cs = slice(x * KP, (x + 1) * KP)
-                nc.tensor.matmul(t[:, cs], lhsT=ones[:], rhs=dc_row[q % 2][:, cs], start=True, stop=True)
-            dcp[q] = t
+            cols = slice(q * 2 * KP, (q + 1) * 2 * KP)
+            nc.sync.dma_start(out=dcb[:, cols], in_=DC[0, cols].partition_broadcast(P))
 
         def load_sv(g):
-            t = work.tile([P, PACK, D], BF16, name="svraw", bufs=4)
+            t = work.tile([P, PACK, D], BF16, name="svraw", bufs=SVB)
             nc.sync.dma_start(out=t[:], in_=sv_v[g])
             svraw[g] = t
 
@@ -81,11 +80,11 @@ def tile_rbf_svm_v_kernel(tc, X, SV, DC, IC, gamma, d2, dec, grad_out, out_0, ou
         gam_raw = keep.tile([P, 1], BF16, name="gam_raw")
         dec_sb = keep.tile([P, GH, PACK], F32, name="dec_sb")
         dc_raw = keep.tile([P, GM, PACK], BF16, name="dc_raw")
-        nc.scalar.dma_start(out=gam_raw[:], in_=gamma.partition_broadcast(P))
+        nc.sync.dma_start(out=gam_raw[:], in_=gamma.partition_broadcast(P))
         nc.scalar.dma_start(out=g_raw[:], in_=grad_out.rearrange("(h p t) -> p h t", p=P, t=PACK))
+        nc.scalar.dma_start(out=dcb[:, 0 : 2 * KP], in_=DC[0, 0 : 2 * KP].partition_broadcast(P))
         nc.gpsimd.dma_start(out=dec_sb[:], in_=dec.rearrange("(h p t) -> p h t", p=P, t=PACK))
         nc.gpsimd.dma_start(out=dc_raw[:], in_=DC[0].rearrange("(g p j) -> p g j", p=P, j=PACK))
-        nc.scalar.dma_start(out=dc_head[:], in_=DC[0, 0 : 2 * KP].partition_broadcast(P))
         load_d2(0, 4)
         x_raw = keep.tile([P, GH, PACK, D], BF16, name="x_raw")
         nc.sync.dma_start(out=x_raw[:, 0], in_=x_v[0])
@@ -101,26 +100,6 @@ def tile_rbf_svm_v_kernel(tc, X, SV, DC, IC, gamma, d2, dec, grad_out, out_0, ou
         nc.scalar.activation(out=warm2[:], in_=warm[:], func=ACT.Ln)
         ident = keep.tile([P, P], F32, name="ident")
         make_identity(nc, ident[:])
-        nc.gpsimd.memset(ones[:], 1.0)
-        nc.gpsimd.memset(dc_row[1][:], 0.0)
-        nc.gpsimd.memset(dc_row[0][:], 0.0)
-        load_dc(1)
-        load_dc(2)
-        ind = keep.tile([P, PACK], F32, name="ind")
-        sel = keep.tile([P, PACK, 32], F32, name="sel")
-        blk = keep.tile([P, PACK], F32, name="blk")
-        nc.vector.tensor_reduce(out=ind[:], in_=ident[:].rearrange("p (q j) -> p j q", j=PACK), axis=mybir.AxisListType.X, op=ALU.add)
-        for b in range(PACK):
-            nc.vector.tensor_reduce(
-                out=sel[:, b],
-                in_=ident[:].rearrange("p (q j) -> p q j", j=PACK),
-                axis=mybir.AxisListType.X,
-                op=ALU.add,
-            )
-
-        nc.vector.tensor_reduce(out=blk[:], in_=ident[:].rearrange("p (b q) -> p b q", b=PACK), axis=mybir.AxisListType.X, op=ALU.add)
-
-
         nt = GH * PACK
         s = keep.tile([P, nt], F32, name="s")
         nc.vector.tensor_scalar(
@@ -136,6 +115,10 @@ def tile_rbf_svm_v_kernel(tc, X, SV, DC, IC, gamma, d2, dec, grad_out, out_0, ou
         nc.vector.tensor_scalar(out=sgn2[:], in0=s[:], scalar1=0.0, scalar2=2.0, op0=ALU.is_ge, op1=ALU.mult)
         sgn = keep.tile([P, nt], F32, name="sgn")
         nc.vector.tensor_scalar(out=sgn[:], in0=sgn2[:], scalar1=-1.0, scalar2=None, op0=ALU.add)
+        flip = keep.tile([P, nt // 2], F32, name="flip")
+        nc.vector.tensor_tensor(out=flip[:], in0=sgn[:, 0::2], in1=sgn[:, 1::2], op=ALU.mult)
+        sgnb = keep.tile([P, nt, P], F32, name="sgnb")
+        nc.vector.tensor_copy(out=sgnb[:], in_=sgn[:].unsqueeze(2).to_broadcast([P, nt, P]))
         ln_s = keep.tile([P, nt], F32, name="ln_s")
         nc.scalar.activation(out=ln_s[:], in_=s_pos[:], func=ACT.Ln)
         nc.scalar.activation(out=warm2[:], in_=warm[:], func=ACT.Exp)
@@ -143,21 +126,12 @@ def tile_rbf_svm_v_kernel(tc, X, SV, DC, IC, gamma, d2, dec, grad_out, out_0, ou
         neg_r = keep.tile([P, nt], F32, name="neg_r")
         neg_s = keep.tile([P, nt], F32, name="neg_s")
         neg_dc = keep.tile([P, GM, PACK], F32, name="neg_dc")
-        ndm = keep.tile([P, GM, PACK, PACK], F32, name="ndm")
         acc = keep.tile([P, nt, D], F32, name="acc")
 
         def constants2():
             nc.vector.tensor_scalar(out=neg_s[:], in0=s[:], scalar1=-1.0, scalar2=None, op0=ALU.mult)
             nc.vector.tensor_tensor(out=neg_r[:], in0=neg_s[:], in1=dec_sb[:].rearrange("p h t -> p (h t)"), op=ALU.mult)
             nc.vector.tensor_scalar(out=neg_dc[:], in0=dc_raw[:], scalar1=-1.0, scalar2=None, op0=ALU.mult)
-
-            nc.vector.tensor_tensor(
-                out=ndm[:],
-                in0=neg_dc[:].unsqueeze(3).to_broadcast([P, GM, PACK, PACK]),
-                in1=blk[:].unsqueeze(1).unsqueeze(1).to_broadcast([P, GM, PACK, PACK]),
-                op=ALU.mult,
-            )
-
 
         def start_acc(i):
             h, t = divmod(i, PACK)
@@ -197,7 +171,7 @@ def tile_rbf_svm_v_kernel(tc, X, SV, DC, IC, gamma, d2, dec, grad_out, out_0, ou
                 t = work.tile([P, D, PACK], BF16, name="grp", align_bytes=64, bufs=2)
                 svg[g] = t
             ds = slice(half * (D // 2), (half + 1) * (D // 2))
-            nc.scalar.copy(
+            (nc.scalar.copy if SVG == "s" else nc.vector.tensor_copy)(
                 out=svg[g][:, ds, :].rearrange("p (c i) j -> p c j i", i=4),
                 in_=svraw[g][:, :, ds].rearrange("p j (c i) -> p c j i", i=4),
             )
@@ -206,6 +180,7 @@ def tile_rbf_svm_v_kernel(tc, X, SV, DC, IC, gamma, d2, dec, grad_out, out_0, ou
             nc.vector.quantize_mx(
                 out=svc[:, g].bitcast(E4), scales=svs[:, g], in_=svg[g][:].rearrange("p d j -> p (d j)")
             )
+            svready[0] += 1
 
         def exp(k):
             h = k % GH
@@ -225,50 +200,40 @@ def tile_rbf_svm_v_kernel(tc, X, SV, DC, IC, gamma, d2, dec, grad_out, out_0, ou
                 nc.vector.tensor_tensor(
                     out=t[:, :, ms, :].rearrange("p j m t -> p m t j"),
                     in0=e[k][:].rearrange("p t (m j) -> p m t j", j=PACK)[:, ms],
-                    in1=dcp[g // 2][:, (g % 2) * KP : (g % 2 + 1) * KP].rearrange("p (m j) -> p m j", j=PACK)[:, ms].unsqueeze(2).to_broadcast([P, 64, PACK, PACK]),
+                    in1=dcb[:, g * KP : (g + 1) * KP].rearrange("p (m j) -> p m j", j=PACK)[:, ms].unsqueeze(2).to_broadcast([P, 64, PACK, PACK]),
                     op=ALU.mult,
                 )
             pb[k] = t
 
-        def sign(k, who):
-            h = k % GH
-            if who == "g" and "g" in SIGN and k < GM * GH - 1:
-                gate = small.tile([P, 1], U32, name="gate")
-                nc.gpsimd.tensor_copy(out=gate[:], in_=pc[k][:, 0:1])
-            for t in range(PACK):
-                i = h * PACK + t
-                if SIGN[t] != who:
-                    continue
-                if who == "g":
-                    nc.gpsimd.tensor_scalar(
-                        out=e[k][:, t, :], in0=e[k][:, t, :], scalar1=sgn[:, i : i + 1], scalar2=0.0, op0=ALU.mult, op1=ALU.add
-                    )
-                elif who == "v":
-                    nc.vector.tensor_scalar(
-                        out=e[k][:, t, :], in0=e[k][:, t, :], scalar1=sgn[:, i : i + 1], scalar2=None, op0=ALU.mult
-                    )
-                else:
-                    nc.scalar.activation(out=e[k][:, t, :], in_=e[k][:, t, :], func=ACT.Copy, scale=sgn[:, i : i + 1])
+        def fold(k, n):
+            b = 2 * n + 1
+            i = (k % GH) * PACK + b
+            if k >= EARLY and n < FOLDS[k]:
+                nc.vector.scalar_tensor_tensor(
+                    out=e[k][:, b, :], in0=e[k][:, b - 1, :], scalar=flip[:, i // 2 : i // 2 + 1], in1=e[k][:, b, :], op0=ALU.mult, op1=ALU.add
+                )
 
         pc, ps = {}, {}
 
         def p_quant(k):
-            c = work.tile([P, KP], U32, name="pc", align_bytes=64, bufs=6)
-            sc = work.tile([P, KP], U8, name="ps", align_bytes=64, bufs=6)
+            c = work.tile([P, KP], U32, name="pc", align_bytes=64, bufs=PCB)
+            sc = work.tile([P, KP], U8, name="ps", align_bytes=64, bufs=PCB)
             nc.vector.quantize_mx(out=c[:].bitcast(E5), scales=sc[:], in_=pb[k][:].rearrange("p j m t -> p (j m t)"))
             pc[k], ps[k] = c, sc
 
         tp = {}
 
-        def turn(k):
+        def turn(k, u):
             words = pb[k][:].rearrange("p j m t -> p (j m t)").bitcast(F32)
-            for u in range(2):
-                t = tpsum.tile([P, PACK, P], F32, name="tp")
-                for j in range(PACK):
-                    nc.tensor.transpose(t[:, j, :], words[:, 2 * P * j + u : 2 * P * (j + 1) : 2], ident[:])
-                tp[k, u] = t
+            t = tpsum.tile([P, PACK, P], F32, name="tp")
+            for j in range(PACK):
+                nc.tensor.transpose(t[:, j, :], words[:, 2 * P * j + u : 2 * P * (j + 1) : 2], ident[:])
+            tp[k, u] = t
 
         pt = {}
+
+        ready = {0: 0, 1: 0}
+        svready = [0]
 
         def evac(k):
             o = work.tile([P, PACK, P, PACK], BF16, name="pt", align_bytes=64, bufs=2)
@@ -283,64 +248,44 @@ def tile_rbf_svm_v_kernel(tc, X, SV, DC, IC, gamma, d2, dec, grad_out, out_0, ou
             nc.vector.quantize_mx(
                 out=ptc[:, k].bitcast(E5), scales=pts[:, k], in_=pt[k][:].rearrange("q t p j -> q (t p j)")
             )
+            ready[k % GH] += 1
 
         cps = {}
 
-        def c_sum(g):
-            t = cpsum.tile([P, PACK, P], F32, name="cps")
-            for b in range(PACK):
-                for i in range(nt):
-                    h, tt = divmod(i, PACK)
-                    nc.tensor.matmul(
-                        t[:, b],
-                        lhsT=e[g * GH + h][:, tt, b * P : (b + 1) * P],
-                        rhs=ident[:],
-                        start=(i == 0),
-                        stop=(i == nt - 1),
-                        is_transpose=True,
-                    )
-            cps[g] = t
+        def c_sum(k, n):
+            g, h = divmod(k, GH)
+            if h == 0 and n == 0:
+                t = cpsum.tile([P, PACK, P], F32, name="cps")
+                cps[g] = t
+            slots = [2 * n + 1] if k >= EARLY and n < FOLDS[k] else [2 * n, 2 * n + 1]
+            for t in slots:
+                nc.tensor.matmul(
+                    cps[g][:].rearrange("p j q -> p (j q)"),
+                    lhsT=sgnb[:, h * PACK + t, :],
+                    rhs=e[k][:, t, :],
+                    start=(h == 0 and n == 0 and t == slots[0]),
+                    stop=(h == GH - 1 and n == 1 and t == slots[-1]),
+                )
 
-        cm = {}
+        crow = {}
 
-        def c_mask(g):
-            cs = small.tile([P, PACK], F32, name="cs")
+        def c_copy(g):
+            t = small.tile([P, KP], F32, name="crow", bufs=2)
             if CRED == "v":
-                nc.vector.tensor_reduce(out=cs[:], in_=cps[g][:], axis=mybir.AxisListType.X, op=ALU.add)
+                nc.vector.tensor_copy(out=t[:], in_=cps[g][:].rearrange("p j q -> p (j q)"))
             else:
-                junk = small.tile([P, P], F32, name="junk", bufs=1)
-                for b in range(PACK):
-                    nc.scalar.activation(out=junk[:], in_=cps[g][:, b], func=ACT.Copy, accum_out=cs[:, b : b + 1])
-            t = small.tile([P, PACK, PACK], F32, name="cm")
-            nc.vector.tensor_tensor(
-                out=t[:],
-                in0=cs[:].unsqueeze(2).to_broadcast([P, PACK, PACK]),
-                in1=ind[:].unsqueeze(1).to_broadcast([P, PACK, PACK]),
-                op=ALU.mult,
-            )
-            cm[g] = t
+                nc.scalar.copy(out=t[:], in_=cps[g][:].rearrange("p j q -> p (j q)"))
+            crow[g] = t
 
-        def c_move(g):
-            nc.tensor.matmul(
-                cps[g][:, 0, 0 : PACK * PACK],
-                lhsT=sel[:].rearrange("p b q -> p (b q)"),
-                rhs=cm[g][:].rearrange("p b j -> p (b j)"),
-                start=True,
-                stop=True,
-            )
+        def c_turn(g):
+            for j in range(PACK):
+                nc.tensor.transpose(cps[g][:, j, :], crow[g][:, j::PACK], ident[:])
 
         negc = {}
 
         def c_neg(g):
-            w = small.tile([P, PACK, PACK], F32, name="cw")
-            nc.vector.tensor_tensor(
-                out=w[:],
-                in0=cps[g][:, 0, 0 : PACK * PACK].rearrange("p (b j) -> p j b", b=PACK),
-                in1=ndm[:, g],
-                op=ALU.mult,
-            )
             t = small.tile([P, PACK], F32, name="negc")
-            nc.vector.tensor_reduce(out=t[:], in_=w[:], axis=mybir.AxisListType.X, op=ALU.add)
+            nc.vector.tensor_tensor(out=t[:], in0=cps[g][:, :, 0], in1=neg_dc[:, g], op=ALU.mult)
             negc[g] = t
 
         m1 = {}
@@ -391,106 +336,77 @@ def tile_rbf_svm_v_kernel(tc, X, SV, DC, IC, gamma, d2, dec, grad_out, out_0, ou
                 )
 
         def sweep(i):
-            if SWEEP[i] == "v":
-                nc.vector.scalar_tensor_tensor(
-                    out=acc[:, i], in0=m0[i][:], scalar=sgn[:, i : i + 1], in1=acc[:, i], op0=ALU.mult, op1=ALU.add
-                )
-            else:
-                w = small.tile([P, D], F32, name="part", bufs=2)
-                nc.scalar.activation(out=w[:], in_=m0[i][:], func=ACT.Copy, scale=sgn[:, i : i + 1])
-                nc.gpsimd.tensor_tensor(out=acc[:, i], in0=acc[:, i], in1=w[:], op=ALU.add)
+            nc.vector.scalar_tensor_tensor(
+                out=acc[:, i], in0=m0[i][:], scalar=sgn[:, i : i + 1], in1=acc[:, i], op0=ALU.mult, op1=ALU.add
+            )
 
         def out0(i):
             h, tt = divmod(i, PACK)
-            o = outs.tile([P, D], F32, name="o0", bufs=4)
-            if OUT0[i] == "v":
-                nc.vector.scalar_tensor_tensor(
-                    out=o[:], in0=m0[i][:], scalar=sgn[:, i : i + 1], in1=acc[:, i], op0=ALU.mult, op1=ALU.add
-                )
-            else:
-                w = small.tile([P, D], F32, name="part", bufs=2)
-                nc.scalar.activation(out=w[:], in_=m0[i][:], func=ACT.Copy, scale=sgn[:, i : i + 1])
-                nc.gpsimd.tensor_tensor(out=o[:], in0=acc[:, i], in1=w[:], op=ALU.add)
+            o = outs.tile([P, D], F32, name="o0", bufs=O0B)
+            nc.vector.scalar_tensor_tensor(
+                out=o[:], in0=m0[i][:], scalar=sgn[:, i : i + 1], in1=acc[:, i], op0=ALU.mult, op1=ALU.add
+            )
             nc.sync.dma_start(out=out0_v[h][:, tt], in_=o[:])
 
         K = GM * GH
-        first = {10: 0, 11: 4, 12: 1, 13: 5, 14: 2, 15: 6, 16: 3, 17: 7}
-        split = {i: (st - 2 - i // PACK) // 2 for st, i in first.items()}
-        early = [0, 1]
+        split = {}
 
-        for st in range(K + 4):
-            odd = st % 2 == 1
-            ga = (st - 4) // 2
-            gb = (st - 5) // 2
-            gc = (st - 3) // 2
-            if st + 3 < K:
-                load_d2(st + 3)
-            if odd and (st + 3) // 2 < GM:
-                load_sv((st + 3) // 2)
-            if st == 6:
-                load_dc(3)
-            if st < K:
-                exp(st)
-            if st == 0:
-                x_group(0)
-                x_quant(0)
-            if st == K + 2:
-                for i in early:
-                    mx0(i, list(range(split[i], GM)), True, True)
-            if not odd and 0 <= ga < GM:
-                c_mask(ga)
-            if st == K + 2:
-                for i in early:
-                    out0(i)
-            if 1 <= st <= K:
-                form_p(st - 1)
-            if st == 1:
-                x_group(1)
-            if st == 2:
-                constants2()
-            if not odd and 0 <= ga < GM:
-                c_move(ga)
-                mx1(ga, 0)
-                mx1(ga, 1)
-            if odd and 0 <= gb < GM:
-                mx1(gb, 2)
-                mx1(gb, 3)
-            if st in first:
-                i = first[st]
+        def pairs(f):
+            def run(n):
+                f(*divmod(n, 2))
+            return run
+
+        def evens(f):
+            def run(n):
+                if n % 2 == 0:
+                    f(n // 2)
+            return run
+
+        def first_sweep(n):
+            if n < nt:
+                i = TILES[n]
+                split[i] = min(ready[i // PACK], svready[0])
                 mx0(i, list(range(split[i])), True, True)
-            if 1 <= st <= K:
-                sign(st - 1, "v")
-            if odd and 0 <= gc < GM:
-                c_sum(gc)
-            if not odd and 0 <= ga < GM:
-                c_neg(ga)
-                out1(ga, 0)
-            if odd and 0 <= gb < GM:
-                out1(gb, 1)
-            if st in first:
-                sweep(first[st])
-            if st % 4 == 0 and 0 < st < K:
-                spread_dc(st // 4)
-            if 1 <= st <= K:
-                turn(st - 1)
-            if 2 <= st <= K + 1:
-                evac(st - 2)
-            if 1 <= st <= K:
-                sign(st - 1, "s")
-            if st == 1:
-                x_quant(1)
-            if 3 <= st < K + 3:
-                pt_quant(st - 3)
-            if odd and 0 <= st - 3 < K:
-                sv_quant((st - 3) // 2)
-            if 1 <= st <= K:
-                p_quant(st - 1)
-                sign(st - 1, "g")
-            if 2 <= st < 2 + nt:
-                start_acc(st - 2)
-            if 0 <= st - 1 < K:
-                sv_group((st - 1) // 2, (st - 1) % 2)
-        for i in range(nt):
-            if i not in early:
-                mx0(i, list(range(split[i], GM)), True, True)
-                out0(i)
+
+        def first_acc(n):
+            if n < nt:
+                sweep(TILES[n])
+
+        def acc0(n):
+            if n < nt:
+                start_acc(TILES[n])
+
+        def load(n):
+            if n >= 3:
+                load_d2(n)
+
+        def loadsv(n):
+            if n % 2 == 0 and n >= 4:
+                load_sv(n // 2)
+
+        def loaddc(n):
+            if n % 4 == 1 and n < 12:
+                load_dc(n // 4 + 1)
+
+        STG = {
+            "load": load, "loadsv": loadsv, "loaddc": loaddc, "exp": exp, "form_p": form_p, "turn0": lambda n: turn(n, 0), "turn1": lambda n: turn(n, 1), "evac": evac,
+            "pt_quant": pt_quant, "p_quant": p_quant, "fold0": lambda n: fold(n, 0), "fold1": lambda n: fold(n, 1),
+            "c_early": lambda n: (c_sum(n, 0), c_sum(n, 1)) if n < EARLY else None,
+            "c_sum0": lambda n: c_sum(n, 0) if n >= EARLY else None, "c_sum1": lambda n: c_sum(n, 1) if n >= EARLY else None,
+            "c_copy": evens(c_copy), "c_turn": evens(c_turn), "c_neg": evens(c_neg),
+            "mx1a": pairs(lambda g, x: mx1(g, 2 * x)), "mx1b": pairs(lambda g, x: mx1(g, 2 * x + 1)),
+            "out1": pairs(out1), "sv_group": pairs(sv_group), "sv_quant": evens(sv_quant),
+            "mx0": first_sweep, "acc": first_acc, "acc0": acc0,
+            "x0": lambda n: (x_group(0), x_quant(0)) if n == 0 else None,
+            "x1": lambda n: (x_group(1), x_quant(1)) if n == 0 else None,
+            "const": lambda n: constants2() if n == 0 else None,
+        }
+        top = max(l for a, l in ORDER) + K
+        for st in range(top):
+            for name, lag in ORDER:
+                n = st - lag
+                if 0 <= n < K:
+                    STG[name](n)
+        for i in LAST:
+            mx0(i, list(range(split[i], GM)), True, True)
+            out0(i)

from contextlib import ExitStack

import concourse.mybir as mybir
from concourse.masks import make_identity

N, M, D = 1024, 4096, 512
P = 128
PACK = 4
KP = P * PACK
GH = N // KP
GM = M // KP
FOLDS = [0] * 3 + [1, 2] * 6 + [2]
TB = 2
AB = 4
CB = 2
EB = 5
PCB = 6
O0B = 4
SVB = 4
EARLY = 1
SVG = "s"
CRED = "s"
ORDER = [("load", -3), ("loaddc", 0), ("c_sum0", 2), ("fold1", 2), ("x1", 3), ("mx1a", 4), ("c_copy", 4), ("sv_group", 4), ("mx1b", 4), ("const", 3), ("x0", 1), ("acc0", 3), ("evac", 2), ("mx0", 9), ("c_turn", 4), ("form_p", 1), ("sv_quant", 5), ("c_sum1", 2), ("exp", 0), ("p_quant", 2), ("c_neg", 4), ("fold0", 1), ("acc", 10), ("out1", 4), ("pt_quant", 3), ("turn0", 1), ("loadsv", -3), ("turn1", 1), ("c_early", 0)]
TILES = [0, 4, 1, 5, 2, 6, 3, 7]
LAST = [0, 1, 2, 3, 4, 5, 6, 7]
FLOPS = 2 * 2 * N * M * D

F32 = mybir.dt.float32
BF16 = mybir.dt.bfloat16
U32 = mybir.dt.uint32
U8 = mybir.dt.uint8
E4 = mybir.dt.float8_e4m3fn_x4
E5 = mybir.dt.float8_e5m2_x4
ALU = mybir.AluOpType
ACT = mybir.ActivationFunctionType


def tile_rbf_svm_v_kernel(tc, X, SV, DC, IC, gamma, d2, dec, grad_out, out_0, out_1):
    nc = tc.nc
    d2_v = d2.rearrange("(h p t) m -> h p t m", p=P, t=PACK)
    x_v = X.rearrange("(h p t) d -> h p t d", p=P, t=PACK)
    sv_v = SV.rearrange("(g p j) d -> g p j d", p=P, j=PACK)
    out0_v = out_0.rearrange("(h p t) d -> h p t d", p=P, t=PACK)
    out1_v = out_1.rearrange("(g p j) d -> g p j d", p=P, j=PACK)

    with ExitStack() as ctx:
        keep = ctx.enter_context(tc.tile_pool(name="keep", bufs=1))
        epool = ctx.enter_context(tc.tile_pool(name="epool", bufs=EB))
        work = ctx.enter_context(tc.tile_pool(name="work", bufs=3))
        outs = ctx.enter_context(tc.tile_pool(name="outs", bufs=2))
        small = ctx.enter_context(tc.tile_pool(name="small", bufs=4))
        tpsum = ctx.enter_context(tc.psum_pool(name="tpsum", bufs=TB))
        cpsum = ctx.enter_context(tc.psum_pool(name="cpsum", bufs=CB))
        apsum = ctx.enter_context(tc.psum_pool(name="apsum", bufs=AB))
        ctx.enter_context(tc.manual_schedule())

        e = {}
        svraw = {}

        def load_d2(k, pieces=1):
            g, h = divmod(k, GH)
            et = epool.tile([P, PACK, KP], F32, name="e")
            step = PACK // pieces
            for i in range(0, PACK, step):
                nc.sync.dma_start(out=et[:, i : i + step, :], in_=d2_v[h][:, i : i + step, g * KP : (g + 1) * KP])
            e[k] = et

        dcb = keep.tile([P, M], BF16, name="dcb")

        def load_dc(q):
            cols = slice(q * 2 * KP, (q + 1) * 2 * KP)
            nc.sync.dma_start(out=dcb[:, cols], in_=DC[0, cols].partition_broadcast(P))

        def load_sv(g):
            t = work.tile([P, PACK, D], BF16, name="svraw", bufs=SVB)
            nc.sync.dma_start(out=t[:], in_=sv_v[g])
            svraw[g] = t

        g_raw = keep.tile([P, GH, PACK], BF16, name="g_raw")
        gam_raw = keep.tile([P, 1], BF16, name="gam_raw")
        dec_sb = keep.tile([P, GH, PACK], F32, name="dec_sb")
        dc_raw = keep.tile([P, GM, PACK], BF16, name="dc_raw")
        nc.sync.dma_start(out=gam_raw[:], in_=gamma.partition_broadcast(P))
        nc.scalar.dma_start(out=g_raw[:], in_=grad_out.rearrange("(h p t) -> p h t", p=P, t=PACK))
        nc.scalar.dma_start(out=dcb[:, 0 : 2 * KP], in_=DC[0, 0 : 2 * KP].partition_broadcast(P))
        nc.gpsimd.dma_start(out=dec_sb[:], in_=dec.rearrange("(h p t) -> p h t", p=P, t=PACK))
        nc.gpsimd.dma_start(out=dc_raw[:], in_=DC[0].rearrange("(g p j) -> p g j", p=P, j=PACK))
        load_d2(0, 4)
        x_raw = keep.tile([P, GH, PACK, D], BF16, name="x_raw")
        nc.sync.dma_start(out=x_raw[:, 0], in_=x_v[0])
        load_d2(1, 2)
        nc.sync.dma_start(out=x_raw[:, 1], in_=x_v[1])
        load_d2(2)
        load_sv(0)
        load_sv(1)

        warm = keep.tile([P, 1], F32, name="warm")
        nc.vector.memset(warm[:], 1.0)
        warm2 = keep.tile([P, 1], F32, name="warm2")
        nc.scalar.activation(out=warm2[:], in_=warm[:], func=ACT.Ln)
        ident = keep.tile([P, P], F32, name="ident")
        make_identity(nc, ident[:])
        nt = GH * PACK
        s = keep.tile([P, nt], F32, name="s")
        nc.vector.tensor_scalar(
            out=s[:], in0=g_raw[:].rearrange("p h t -> p (h t)"), scalar1=gam_raw[:, 0:1], scalar2=2.0, op0=ALU.mult, op1=ALU.mult
        )
        s_abs = keep.tile([P, nt], F32, name="s_abs")
        nc.vector.scalar_tensor_tensor(out=s_abs[:], in0=s[:], scalar=-1.0, in1=s[:], op0=ALU.mult, op1=ALU.max)
        neg_gam = keep.tile([P, 1], F32, name="neg_gam")
        nc.vector.tensor_scalar(out=neg_gam[:], in0=gam_raw[:], scalar1=-1.0, scalar2=None, op0=ALU.mult)
        s_pos = keep.tile([P, nt], F32, name="s_pos")
        nc.vector.tensor_scalar(out=s_pos[:], in0=s_abs[:], scalar1=1e-19, scalar2=None, op0=ALU.max)
        sgn2 = keep.tile([P, nt], F32, name="sgn2")
        nc.vector.tensor_scalar(out=sgn2[:], in0=s[:], scalar1=0.0, scalar2=2.0, op0=ALU.is_ge, op1=ALU.mult)
        sgn = keep.tile([P, nt], F32, name="sgn")
        nc.vector.tensor_scalar(out=sgn[:], in0=sgn2[:], scalar1=-1.0, scalar2=None, op0=ALU.add)
        flip = keep.tile([P, nt // 2], F32, name="flip")
        nc.vector.tensor_tensor(out=flip[:], in0=sgn[:, 0::2], in1=sgn[:, 1::2], op=ALU.mult)
        sgnb = keep.tile([P, nt, P], F32, name="sgnb")
        nc.vector.tensor_copy(out=sgnb[:], in_=sgn[:].unsqueeze(2).to_broadcast([P, nt, P]))
        ln_s = keep.tile([P, nt], F32, name="ln_s")
        nc.scalar.activation(out=ln_s[:], in_=s_pos[:], func=ACT.Ln)
        nc.scalar.activation(out=warm2[:], in_=warm[:], func=ACT.Exp)

        neg_r = keep.tile([P, nt], F32, name="neg_r")
        neg_s = keep.tile([P, nt], F32, name="neg_s")
        neg_dc = keep.tile([P, GM, PACK], F32, name="neg_dc")
        acc = keep.tile([P, nt, D], F32, name="acc")

        def constants2():
            nc.vector.tensor_scalar(out=neg_s[:], in0=s[:], scalar1=-1.0, scalar2=None, op0=ALU.mult)
            nc.vector.tensor_tensor(out=neg_r[:], in0=neg_s[:], in1=dec_sb[:].rearrange("p h t -> p (h t)"), op=ALU.mult)
            nc.vector.tensor_scalar(out=neg_dc[:], in0=dc_raw[:], scalar1=-1.0, scalar2=None, op0=ALU.mult)

        def start_acc(i):
            h, t = divmod(i, PACK)
            nc.gpsimd.tensor_scalar(
                out=acc[:, i], in0=x_raw[:, h, t], scalar1=neg_r[:, i : i + 1], scalar2=0.0, op0=ALU.mult, op1=ALU.add
            )


        xc = keep.tile([P, GH, D], U32, name="xc", align_bytes=64)
        xs = keep.tile([P, GH, D], U8, name="xs", align_bytes=64)
        svc = keep.tile([P, GM, D], U32, name="svc", align_bytes=64)
        svs = keep.tile([P, GM, D], U8, name="svs", align_bytes=64)
        ptc = keep.tile([P, GM * GH, KP], U32, name="ptc", align_bytes=64)
        pts = keep.tile([P, GM * GH, KP], U8, name="pts", align_bytes=64)

        xg = {}

        def x_group(h):
            t = work.tile([P, D, PACK], BF16, name="xg", align_bytes=64, bufs=1)
            nc.vector.tensor_tensor(
                out=t[:].rearrange("p (c i) t -> p c t i", i=4),
                in0=x_raw[:, h].rearrange("p t (c i) -> p c t i", i=4),
                in1=sgn[:, h * PACK : (h + 1) * PACK].unsqueeze(1).unsqueeze(3).to_broadcast([P, D // 4, PACK, 4]),
                op=ALU.mult,
            )
            xg[h] = t

        def x_quant(h):
            nc.vector.quantize_mx(
                out=xc[:, h].bitcast(E4), scales=xs[:, h], in_=xg[h][:].rearrange("p d t -> p (d t)")
            )

        svg = {}

        def sv_group(g, half):
            if half == 0:
                t = work.tile([P, D, PACK], BF16, name="grp", align_bytes=64, bufs=2)
                svg[g] = t
            ds = slice(half * (D // 2), (half + 1) * (D // 2))
            (nc.scalar.copy if SVG == "s" else nc.vector.tensor_copy)(
                out=svg[g][:, ds, :].rearrange("p (c i) j -> p c j i", i=4),
                in_=svraw[g][:, :, ds].rearrange("p j (c i) -> p c j i", i=4),
            )

        def sv_quant(g):
            nc.vector.quantize_mx(
                out=svc[:, g].bitcast(E4), scales=svs[:, g], in_=svg[g][:].rearrange("p d j -> p (d j)")
            )
            svready[0] += 1

        def exp(k):
            h = k % GH
            for t in range(PACK):
                i = h * PACK + t
                nc.scalar.activation(
                    out=e[k][:, t, :], in_=e[k][:, t, :], func=ACT.Exp, scale=neg_gam[:, 0:1], bias=ln_s[:, i : i + 1]
                )

        pb = {}

        def form_p(k):
            g = k // GH
            t = work.tile([P, PACK, P, PACK], BF16, name="pb", align_bytes=64)
            for q in range(2):
                ms = slice(q * 64, (q + 1) * 64)
                nc.vector.tensor_tensor(
                    out=t[:, :, ms, :].rearrange("p j m t -> p m t j"),
                    in0=e[k][:].rearrange("p t (m j) -> p m t j", j=PACK)[:, ms],
                    in1=dcb[:, g * KP : (g + 1) * KP].rearrange("p (m j) -> p m j", j=PACK)[:, ms].unsqueeze(2).to_broadcast([P, 64, PACK, PACK]),
                    op=ALU.mult,
                )
            pb[k] = t

        def fold(k, n):
            b = 2 * n + 1
            i = (k % GH) * PACK + b
            if k >= EARLY and n < FOLDS[k]:
                nc.vector.scalar_tensor_tensor(
                    out=e[k][:, b, :], in0=e[k][:, b - 1, :], scalar=flip[:, i // 2 : i // 2 + 1], in1=e[k][:, b, :], op0=ALU.mult, op1=ALU.add
                )

        pc, ps = {}, {}

        def p_quant(k):
            c = work.tile([P, KP], U32, name="pc", align_bytes=64, bufs=PCB)
            sc = work.tile([P, KP], U8, name="ps", align_bytes=64, bufs=PCB)
            nc.vector.quantize_mx(out=c[:].bitcast(E5), scales=sc[:], in_=pb[k][:].rearrange("p j m t -> p (j m t)"))
            pc[k], ps[k] = c, sc

        tp = {}

        def turn(k, u):
            words = pb[k][:].rearrange("p j m t -> p (j m t)").bitcast(F32)
            t = tpsum.tile([P, PACK, P], F32, name="tp")
            for j in range(PACK):
                nc.tensor.transpose(t[:, j, :], words[:, 2 * P * j + u : 2 * P * (j + 1) : 2], ident[:])
            tp[k, u] = t

        pt = {}

        ready = {0: 0, 1: 0}
        svready = [0]

        def evac(k):
            o = work.tile([P, PACK, P, PACK], BF16, name="pt", align_bytes=64, bufs=2)
            for u in range(2):
                nc.scalar.copy(
                    out=o[:, 2 * u : 2 * u + 2],
                    in_=tp[k, u][:].rearrange("q j p -> q (j p)").bitcast(BF16).rearrange("q (j p e) -> q e p j", j=PACK, e=2),
                )
            pt[k] = o

        def pt_quant(k):
            nc.vector.quantize_mx(
                out=ptc[:, k].bitcast(E5), scales=pts[:, k], in_=pt[k][:].rearrange("q t p j -> q (t p j)")
            )
            ready[k % GH] += 1

        cps = {}

        def c_sum(k, n):
            g, h = divmod(k, GH)
            if h == 0 and n == 0:
                t = cpsum.tile([P, PACK, P], F32, name="cps")
                cps[g] = t
            slots = [2 * n + 1] if k >= EARLY and n < FOLDS[k] else [2 * n, 2 * n + 1]
            for t in slots:
                nc.tensor.matmul(
                    cps[g][:].rearrange("p j q -> p (j q)"),
                    lhsT=sgnb[:, h * PACK + t, :],
                    rhs=e[k][:, t, :],
                    start=(h == 0 and n == 0 and t == slots[0]),
                    stop=(h == GH - 1 and n == 1 and t == slots[-1]),
                )

        crow = {}

        def c_copy(g):
            t = small.tile([P, KP], F32, name="crow", bufs=2)
            if CRED == "v":
                nc.vector.tensor_copy(out=t[:], in_=cps[g][:].rearrange("p j q -> p (j q)"))
            else:
                nc.scalar.copy(out=t[:], in_=cps[g][:].rearrange("p j q -> p (j q)"))
            crow[g] = t

        def c_turn(g):
            for j in range(PACK):
                nc.tensor.transpose(cps[g][:, j, :], crow[g][:, j::PACK], ident[:])

        negc = {}

        def c_neg(g):
            t = small.tile([P, PACK], F32, name="negc")
            nc.vector.tensor_tensor(out=t[:], in0=cps[g][:, :, 0], in1=neg_dc[:, g], op=ALU.mult)
            negc[g] = t

        m1 = {}

        def mx1(g, j):
            t = apsum.tile([P, D], F32, name="bank")
            js = slice(j * P, (j + 1) * P)
            for h in range(GH):
                k = g * GH + h
                nc.tensor.matmul_mx(
                    out=t[:],
                    lhsT=pc[k][:, js].bitcast(E5),
                    lhsT_scale=ps[k][:, js],
                    rhs=xc[:, h].bitcast(E4),
                    rhs_scale=xs[:, h],
                    start=(h == 0),
                    stop=(h == GH - 1),
                )
            m1[g, j] = t

        def out1(g, pair):
            o = outs.tile([P, 2, D], F32, name="o1")
            for x in range(2):
                j = 2 * pair + x
                nc.vector.scalar_tensor_tensor(
                    out=o[:, x], in0=svraw[g][:, j], scalar=negc[g][:, j : j + 1], in1=m1[g, j][:], op0=ALU.mult, op1=ALU.add
                )
            nc.sync.dma_start(out=out1_v[g][:, 2 * pair : 2 * pair + 2], in_=o[:])

        m0 = {}

        def mx0(i, gs, start, stop):
            h, tt = divmod(i, PACK)
            if start:
                t = apsum.tile([P, D], F32, name="bank")
                m0[i] = t
            ts = slice(tt * P, (tt + 1) * P)
            for n, g in enumerate(gs):
                k = g * GH + h
                nc.tensor.matmul_mx(
                    out=m0[i][:],
                    lhsT=ptc[:, k, ts].bitcast(E5),
                    lhsT_scale=pts[:, k, ts],
                    rhs=svc[:, g].bitcast(E4),
                    rhs_scale=svs[:, g],
                    start=(start and n == 0),
                    stop=(stop and n == len(gs) - 1),
                )

        def sweep(i):
            nc.vector.scalar_tensor_tensor(
                out=acc[:, i], in0=m0[i][:], scalar=sgn[:, i : i + 1], in1=acc[:, i], op0=ALU.mult, op1=ALU.add
            )

        def out0(i):
            h, tt = divmod(i, PACK)
            o = outs.tile([P, D], F32, name="o0", bufs=O0B)
            nc.vector.scalar_tensor_tensor(
                out=o[:], in0=m0[i][:], scalar=sgn[:, i : i + 1], in1=acc[:, i], op0=ALU.mult, op1=ALU.add
            )
            nc.sync.dma_start(out=out0_v[h][:, tt], in_=o[:])

        K = GM * GH
        split = {}

        def pairs(f):
            def run(n):
                f(*divmod(n, 2))
            return run

        def evens(f):
            def run(n):
                if n % 2 == 0:
                    f(n // 2)
            return run

        def first_sweep(n):
            if n < nt:
                i = TILES[n]
                split[i] = min(ready[i // PACK], svready[0])
                mx0(i, list(range(split[i])), True, True)

        def first_acc(n):
            if n < nt:
                sweep(TILES[n])

        def acc0(n):
            if n < nt:
                start_acc(TILES[n])

        def load(n):
            if n >= 3:
                load_d2(n)

        def loadsv(n):
            if n % 2 == 0 and n >= 4:
                load_sv(n // 2)

        def loaddc(n):
            if n % 4 == 1 and n < 12:
                load_dc(n // 4 + 1)

        STG = {
            "load": load, "loadsv": loadsv, "loaddc": loaddc, "exp": exp, "form_p": form_p, "turn0": lambda n: turn(n, 0), "turn1": lambda n: turn(n, 1), "evac": evac,
            "pt_quant": pt_quant, "p_quant": p_quant, "fold0": lambda n: fold(n, 0), "fold1": lambda n: fold(n, 1),
            "c_early": lambda n: (c_sum(n, 0), c_sum(n, 1)) if n < EARLY else None,
            "c_sum0": lambda n: c_sum(n, 0) if n >= EARLY else None, "c_sum1": lambda n: c_sum(n, 1) if n >= EARLY else None,
            "c_copy": evens(c_copy), "c_turn": evens(c_turn), "c_neg": evens(c_neg),
            "mx1a": pairs(lambda g, x: mx1(g, 2 * x)), "mx1b": pairs(lambda g, x: mx1(g, 2 * x + 1)),
            "out1": pairs(out1), "sv_group": pairs(sv_group), "sv_quant": evens(sv_quant),
            "mx0": first_sweep, "acc": first_acc, "acc0": acc0,
            "x0": lambda n: (x_group(0), x_quant(0)) if n == 0 else None,
            "x1": lambda n: (x_group(1), x_quant(1)) if n == 0 else None,
            "const": lambda n: constants2() if n == 0 else None,
        }
        top = max(l for a, l in ORDER) + K
        for st in range(top):
            for name, lag in ORDER:
                n = st - lag
                if 0 <= n < K:
                    STG[name](n)
        for i in LAST:
            mx0(i, list(range(split[i], GM)), True, True)
            out0(i)
